import numpy as np
import ml_dtypes


def mxq(x, axis, fmt="e4m3"):
    dtype, down = {"e4m3": (ml_dtypes.float8_e4m3fn, 7), "e5m2": (ml_dtypes.float8_e5m2, 14)}[fmt]
    v = np.moveaxis(np.asarray(x, np.float32).astype(ml_dtypes.bfloat16).astype(np.float64), axis, -1)
    blocks = v.reshape(v.shape[:-1] + (-1, 32))
    amax = np.abs(blocks).max(-1, keepdims=True)
    byte = np.maximum(np.where(amax > 0, np.frexp(amax)[1] - 1 + 127, 0) - down, 1)
    scale = np.exp2(byte - 127.0)
    codes = (blocks / scale).astype(np.float32).astype(dtype).astype(np.float64)
    return np.moveaxis((codes * scale).reshape(v.shape), -1, axis)


WIDE = False


def mx_kscale(k):
    if not WIDE:
        return np.ones(k)
    levels = np.array([10, -10, 5, -5, 0])
    if k % 512:
        return np.exp2(np.random.permutation(np.resize(levels, k // 32))).repeat(32)
    a = np.empty((k // 512, 16))
    for p in range(k // 512):
        a[p, :8] = np.random.permutation(np.resize(levels, 8))
        for g in range(8):
            far = levels[np.abs(levels - a[p, g]) >= 10]
            a[p, g + 8] = far[np.random.randint(len(far))]
    return np.exp2(a.ravel()).repeat(32)


BF16 = ml_dtypes.bfloat16


def bf(x):
    return np.asarray(x, np.float32).astype(BF16)


def f64(x):
    return np.asarray(x).astype(np.float64)


B, IN, H, OUT, L, STEPS = 1024, 512, 1024, 128, 3, 3
LN_EPS = 1e-5


def layer_norm(v, g, b):
    m = v.mean(-1, keepdims=True)
    var = ((v - m) ** 2).mean(-1, keepdims=True)
    return (v - m) / np.sqrt(var + LN_EPS) * g + b


def setup_inputs():
    s = mx_kscale(H)
    s = s / s.max()
    return {"h": bf(np.random.standard_normal((B, H)) * s),
            "W_liq": bf(np.random.standard_normal((L, H, H)) / np.sqrt(H) / s),
            "b_liq": bf(np.random.standard_normal((L, H)) * 0.3),
            "g_liq": bf(1.0 + 0.1 * np.random.standard_normal((L, H))),
            "beta_liq": bf(np.random.standard_normal((L, H)) * 0.3)}


def reference(h, W_liq, b_liq, g_liq, beta_liq):
    h = f64(h)
    lin = mxq(h, 1, "e4m3") @ mxq(f64(W_liq), 2, "e4m3").transpose(0, 2, 1)
    pre = h[None] + lin + f64(b_liq)[:, None, :]
    return layer_norm(pre, f64(g_liq)[:, None, :], f64(beta_liq)[:, None, :]).sum(0)

@@ -1,0 +1,220 @@
+from contextlib import ExitStack
+
+import concourse.mybir as mybir
+from concourse.masks import make_identity
+
+F32 = mybir.dt.float32
+BF16 = mybir.dt.bfloat16
+U32 = mybir.dt.uint32
+U8 = mybir.dt.uint8
+I32 = mybir.dt.int32
+FP8X4 = mybir.dt.float8_e4m3fn_x4
+ADD = mybir.AluOpType.add
+MULT = mybir.AluOpType.mult
+ACT = mybir.ActivationFunctionType
+
+P = 128
+B = 1024
+H = 1024
+L = 3
+LN_EPS = 1e-5
+PACK = 4
+K_PASS = P * PACK
+PASSES = H // K_PASS
+BANK = 512
+HALVES = H // BANK
+UNIT_TILES = 4
+UNIT_ROWS = UNIT_TILES * P
+UNITS = B // UNIT_ROWS
+N_TILES = H // P
+BANK_TILES = BANK // P
+
+FLOPS = 2 * L * B * H * H
+
+
+def tile_advancedliquidneuralnetwork_pa_kernel(tc, h, W_liq, b_liq, g_liq, beta_liq, out):
+    nc = tc.nc
+    with ExitStack() as ctx:
+        const = ctx.enter_context(tc.tile_pool(name="const", bufs=1))
+        raw_pool = ctx.enter_context(tc.tile_pool(name="raw", bufs=1))
+        stage = ctx.enter_context(tc.tile_pool(name="stage", bufs=3))
+        keep = ctx.enter_context(tc.tile_pool(name="keep", bufs=1))
+        work = ctx.enter_context(tc.tile_pool(name="work", bufs=4))
+        z_pool = ctx.enter_context(tc.tile_pool(name="z", bufs=2 * UNIT_TILES))
+        acc_pool = ctx.enter_context(tc.tile_pool(name="acc", bufs=1))
+        out_pool = ctx.enter_context(tc.tile_pool(name="result", bufs=2))
+        stats = ctx.enter_context(tc.tile_pool(name="stats", bufs=8))
+        psum = ctx.enter_context(tc.psum_pool(name="psum", bufs=4))
+
+        def load_unit(name, slots, dram_rows):
+            raw = raw_pool.tile([P, UNIT_TILES, H], BF16, name=name, bufs=slots)
+            nc.sync.dma_start(out=raw[:], in_=dram_rows.rearrange("(j p) k -> p j k", p=P))
+            return raw
+
+        def unit_rows(u):
+            return slice(u * UNIT_ROWS, (u + 1) * UNIT_ROWS)
+
+        h_raw = [None] * UNITS
+        w_raw = {}
+        h_raw[0] = load_unit("h_raw", UNITS, h[unit_rows(0), :])
+        rows = const.tile([P, H], BF16)
+        nc.vector.memset(rows[:].bitcast(I32), 0)
+        nc.sync.dma_start(out=rows[0:L, :], in_=b_liq)
+        nc.sync.dma_start(out=rows[L : 2 * L, :], in_=g_liq)
+        nc.sync.dma_start(out=rows[2 * L : 3 * L, :], in_=beta_liq)
+        for l in range(L):
+            for u in range(UNITS):
+                w_raw[(l, u)] = load_unit("w_raw", 4, W_liq[l, unit_rows(u), :])
+        h_raw[1] = load_unit("h_raw", UNITS, h[unit_rows(1), :])
+
+        ident_f32 = const.tile([P, P], F32)
+        make_identity(nc, ident_f32[:])
+        ident_bf16 = const.tile([P, P], BF16)
+        make_identity(nc, ident_bf16[:])
+        eps = const.tile([P, 1], F32)
+        nc.vector.memset(eps[:], LN_EPS)
+        warm = const.tile([P, 1], F32)
+        nc.scalar.activation(out=warm[:], in_=eps[:], func=ACT.Sqrt)
+
+        h_codes = keep.tile([P, PASSES, B], U32, align_bytes=64)
+        h_scales = keep.tile([P, PASSES, B], U8, align_bytes=64)
+        w_codes = keep.tile([P, L, PASSES, H], U32, align_bytes=64)
+        w_scales = keep.tile([P, L, PASSES, H], U8, align_bytes=64)
+
+        def quantise_unit(raw, codes, scales):
+            grouped = stage.tile([P, PASSES, UNIT_TILES, P, PACK], BF16, align_bytes=64)
+            grouped_words = grouped[:].bitcast(F32)
+            for j in range(UNIT_TILES):
+                raw_words = raw[:, j, :].bitcast(F32)
+                flipped = psum.tile([P, PASSES, 2, P], F32, tag="t")
+                for c in range(PASSES):
+                    for w in range(2):
+                        first = 2 * c * P + w
+                        nc.tensor.transpose(
+                            flipped[:, c, w, :], raw_words[:, first : 2 * (c + 1) * P : 2], ident_f32[:]
+                        )
+                nc.scalar.copy(out=grouped_words[:, :, j, :, :], in_=flipped[:].rearrange("p c w r -> p c r w"))
+            for c in range(PASSES):
+                nc.vector.quantize_mx(
+                    out=codes[:, c, :].bitcast(FP8X4),
+                    scales=scales[:, c, :],
+                    in_=grouped[:, c].rearrange("p j r t -> p (j r t)"),
+                )
+
+        def quantise_h(u):
+            quantise_unit(h_raw[u], h_codes[:, :, unit_rows(u)], h_scales[:, :, unit_rows(u)])
+
+        def quantise_w(l):
+            for u in range(UNITS):
+                quantise_unit(w_raw[(l, u)], w_codes[:, l, :, unit_rows(u)], w_scales[:, l, :, unit_rows(u)])
+
+        quantise_h(0)
+
+        bias_bc = const.tile([P, L, H], BF16)
+        for l in range(L):
+            for half in range(HALVES):
+                cols = slice(half * BANK, (half + 1) * BANK)
+                spread = psum.tile([P, BANK], F32, tag="t")
+                nc.tensor.matmul(
+                    out=spread[:], lhsT=ident_bf16[:, l : l + 1].to_broadcast([P, P]), rhs=rows[:, cols],
+                    start=True, stop=True,
+                )
+                nc.scalar.copy(out=bias_bc[:, l, cols], in_=spread[:])
+        rows_T = psum.tile([P, N_TILES, P], BF16, tag="t")
+        for t in range(N_TILES):
+            nc.tensor.transpose(rows_T[:, t, :], rows[:, t * P : (t + 1) * P], ident_bf16[:])
+        params_T = const.tile([P, N_TILES, 3 * L], F32)
+        nc.vector.tensor_copy(out=params_T[:], in_=rows_T[:, :, 0 : 3 * L])
+        shift_T = const.tile([P, N_TILES], F32)
+        nc.vector.tensor_reduce(out=shift_T[:], in_=params_T[:, :, 2 * L : 3 * L], axis=mybir.AxisListType.X, op=ADD)
+
+        def normalised_branch(l, u, j):
+            tile_cols = slice((u * UNIT_TILES + j) * P, (u * UNIT_TILES + j + 1) * P)
+            resid = work.tile([P, H], F32, bufs=6)
+            nc.vector.tensor_tensor(out=resid[:], in0=h_raw[u][:, j, :], in1=bias_bc[:, l, :], op=ADD)
+            pre = work.tile([P, H], F32)
+            row_sum = stats.tile([P, HALVES], F32)
+            for half in range(HALVES):
+                cols = slice(half * BANK, (half + 1) * BANK)
+                product = psum.tile([P, BANK], F32, tag="x")
+                for c in range(PASSES):
+                    nc.tensor.matmul_mx(
+                        out=product[:],
+                        lhsT=h_codes[:, c, tile_cols].bitcast(FP8X4),
+                        lhsT_scale=h_scales[:, c, tile_cols],
+                        rhs=w_codes[:, l, c, cols].bitcast(FP8X4),
+                        rhs_scale=w_scales[:, l, c, cols],
+                        start=(c == 0),
+                        stop=(c == PASSES - 1),
+                    )
+                nc.vector.scalar_tensor_tensor(
+                    out=pre[:, cols], in0=resid[:, cols], scalar=0.0, in1=product[:],
+                    op0=ADD, op1=ADD, accum_out=row_sum[:, half : half + 1],
+                )
+            neg_mean = stats.tile([P, 1], F32)
+            nc.vector.tensor_scalar(
+                out=neg_mean[:], in0=row_sum[:, 0:1], scalar1=row_sum[:, 1:2], scalar2=-1.0 / H, op0=ADD, op1=MULT
+            )
+            z = z_pool.tile([P, H], F32)
+            sum_sq = stats.tile([P, 1], F32)
+            nc.scalar.activation(out=z[:], in_=pre[:], func=ACT.Square, bias=neg_mean[:], scale=1.0, accum_out=sum_sq[:])
+            std = stats.tile([P, 1], F32)
+            nc.scalar.activation(out=std[:], in_=sum_sq[:], func=ACT.Sqrt, bias=eps[:], scale=1.0 / H)
+            rstd = stats.tile([P, 1], F32)
+            nc.vector.reciprocal(rstd[:], std[:])
+            nc.gpsimd.tensor_scalar(out=z[:], in0=pre[:], scalar1=neg_mean[:], scalar2=rstd[:], op0=ADD, op1=MULT)
+            return z
+
+        def add_branch(l, zs, acc_T):
+            for t in range(N_TILES):
+                z_T = psum.tile([P, UNIT_TILES, P], F32, tag="t")
+                for j in range(UNIT_TILES):
+                    nc.tensor.transpose(z_T[:, j, :], zs[j][:, t * P : (t + 1) * P], ident_f32[:])
+                z_T_cols = z_T[:].rearrange("p j r -> p (j r)")
+                gain = params_T[:, t, L + l : L + l + 1]
+                if l == 0:
+                    nc.scalar.activation(
+                        out=acc_T[:, t, :], in_=z_T_cols, func=ACT.Identity, bias=shift_T[:, t : t + 1], scale=gain
+                    )
+                else:
+                    nc.vector.scalar_tensor_tensor(
+                        out=acc_T[:, t, :], in0=z_T_cols, scalar=gain, in1=acc_T[:, t, :], op0=MULT, op1=ADD
+                    )
+
+        def store_unit(u, acc_T):
+            for j in range(UNIT_TILES):
+                result = out_pool.tile([P, H], F32)
+                for half in range(HALVES):
+                    rows_back = psum.tile([P, BANK_TILES, P], F32, tag="t")
+                    for t in range(BANK_TILES):
+                        nc.tensor.transpose(
+                            rows_back[:, t, :], acc_T[:, half * BANK_TILES + t, j * P : (j + 1) * P], ident_f32[:]
+                        )
+                    nc.scalar.copy(
+                        out=result[:, half * BANK : (half + 1) * BANK], in_=rows_back[:].rearrange("p t n -> p (t n)")
+                    )
+                first = (u * UNIT_TILES + j) * P
+                nc.sync.dma_start(out=out[first : first + P, :], in_=result[:])
+
+        acc_Ts = {}
+
+        def finish(u, l, zs):
+            if l == 0:
+                acc_Ts[u] = acc_pool.tile([P, N_TILES, UNIT_ROWS], F32, name="acc_T")
+            add_branch(l, zs, acc_Ts[u])
+            if l == L - 1:
+                store_unit(u, acc_Ts[u])
+
+        quantise_w(0)
+        waiting = None
+        for u in range(UNITS):
+            for l in range(L):
+                if u == 0 and l + 1 < L:
+                    quantise_w(l + 1)
+                if u + 1 < UNITS and l == L - 1:
+                    quantise_h(u + 1)
+                zs = [normalised_branch(l, u, j) for j in range(UNIT_TILES)]
+                if waiting is not None:
+                    finish(*waiting)
+                waiting = (u, l, zs)
+        finish(*waiting)

@@ -37,18 +37,20 @@ def tile_advancedliquidneuralnetwork_pa_kernel(tc, h, W_liq, b_liq, g_liq, beta_
     with ExitStack() as ctx:
         const = ctx.enter_context(tc.tile_pool(name="const", bufs=1))
         raw_pool = ctx.enter_context(tc.tile_pool(name="raw", bufs=1))
-        stage = ctx.enter_context(tc.tile_pool(name="stage", bufs=3))
+        stage = ctx.enter_context(tc.tile_pool(name="stage", bufs=2))
         keep = ctx.enter_context(tc.tile_pool(name="keep", bufs=1))
-        work = ctx.enter_context(tc.tile_pool(name="work", bufs=4))
-        z_pool = ctx.enter_context(tc.tile_pool(name="z", bufs=2 * UNIT_TILES))
-        acc_pool = ctx.enter_context(tc.tile_pool(name="acc", bufs=1))
-        out_pool = ctx.enter_context(tc.tile_pool(name="result", bufs=2))
+        work = ctx.enter_context(tc.tile_pool(name="work", bufs=1))
+        gained = ctx.enter_context(tc.tile_pool(name="gained", bufs=2))
+        out_pool = ctx.enter_context(tc.tile_pool(name="result", bufs=3))
         stats = ctx.enter_context(tc.tile_pool(name="stats", bufs=8))
         psum = ctx.enter_context(tc.psum_pool(name="psum", bufs=4))
 
-        def load_unit(name, slots, dram_rows):
+        def load_unit(name, slots, dram_rows, pieces):
             raw = raw_pool.tile([P, UNIT_TILES, H], BF16, name=name, bufs=slots)
-            nc.sync.dma_start(out=raw[:], in_=dram_rows.rearrange("(j p) k -> p j k", p=P))
+            source = dram_rows.rearrange("(j p) k -> p j k", p=P)
+            step = UNIT_TILES // pieces
+            for first in range(0, UNIT_TILES, step):
+                nc.sync.dma_start(out=raw[:, first : first + step, :], in_=source[:, first : first + step, :])
             return raw
 
         def unit_rows(u):
@@ -56,16 +58,17 @@ def tile_advancedliquidneuralnetwork_pa_kernel(tc, h, W_liq, b_liq, g_liq, beta_
 
         h_raw = [None] * UNITS
         w_raw = {}
-        h_raw[0] = load_unit("h_raw", UNITS, h[unit_rows(0), :])
+        h_raw[0] = load_unit("h_raw", UNITS, h[unit_rows(0), :], 2)
         rows = const.tile([P, H], BF16)
         nc.vector.memset(rows[:].bitcast(I32), 0)
         nc.sync.dma_start(out=rows[0:L, :], in_=b_liq)
         nc.sync.dma_start(out=rows[L : 2 * L, :], in_=g_liq)
         nc.sync.dma_start(out=rows[2 * L : 3 * L, :], in_=beta_liq)
         for l in range(L):
+            if l == L - 1:
+                h_raw[1] = load_unit("h_raw", UNITS, h[unit_rows(1), :], 1)
             for u in range(UNITS):
-                w_raw[(l, u)] = load_unit("w_raw", 4, W_liq[l, unit_rows(u), :])
-        h_raw[1] = load_unit("h_raw", UNITS, h[unit_rows(1), :])
+                w_raw[(l, u)] = load_unit("w_raw", 3, W_liq[l, unit_rows(u), :], 2 if l == 0 else 1)
 
         ident_f32 = const.tile([P, P], F32)
         make_identity(nc, ident_f32[:])
@@ -74,14 +77,14 @@ def tile_advancedliquidneuralnetwork_pa_kernel(tc, h, W_liq, b_liq, g_liq, beta_
         eps = const.tile([P, 1], F32)
         nc.vector.memset(eps[:], LN_EPS)
         warm = const.tile([P, 1], F32)
-        nc.scalar.activation(out=warm[:], in_=eps[:], func=ACT.Sqrt)
+        nc.scalar.activation(out=warm[:], in_=eps[:], func=ACT.Abs_reciprocal_sqrt)
 
         h_codes = keep.tile([P, PASSES, B], U32, align_bytes=64)
         h_scales = keep.tile([P, PASSES, B], U8, align_bytes=64)
         w_codes = keep.tile([P, L, PASSES, H], U32, align_bytes=64)
         w_scales = keep.tile([P, L, PASSES, H], U8, align_bytes=64)
 
-        def quantise_unit(raw, codes, scales):
+        def quantise_unit(raw, codes, scales, engines):
             grouped = stage.tile([P, PASSES, UNIT_TILES, P, PACK], BF16, align_bytes=64)
             grouped_words = grouped[:].bitcast(F32)
             for j in range(UNIT_TILES):
@@ -93,7 +96,11 @@ def tile_advancedliquidneuralnetwork_pa_kernel(tc, h, W_liq, b_liq, g_liq, beta_
                         nc.tensor.transpose(
                             flipped[:, c, w, :], raw_words[:, first : 2 * (c + 1) * P : 2], ident_f32[:]
                         )
-                nc.scalar.copy(out=grouped_words[:, :, j, :, :], in_=flipped[:].rearrange("p c w r -> p c r w"))
+                words = flipped[:].rearrange("p c w r -> p c r w")
+                if engines[j % 2] == "vector":
+                    nc.vector.tensor_copy(out=grouped_words[:, :, j, :, :], in_=words)
+                else:
+                    nc.scalar.copy(out=grouped_words[:, :, j, :, :], in_=words)
             for c in range(PASSES):
                 nc.vector.quantize_mx(
                     out=codes[:, c, :].bitcast(FP8X4),
@@ -101,25 +108,32 @@ def tile_advancedliquidneuralnetwork_pa_kernel(tc, h, W_liq, b_liq, g_liq, beta_
                     in_=grouped[:, c].rearrange("p j r t -> p (j r t)"),
                 )
 
-        def quantise_h(u):
-            quantise_unit(h_raw[u], h_codes[:, :, unit_rows(u)], h_scales[:, :, unit_rows(u)])
+        def quantise_h(u, engines=("scalar", "scalar")):
+            quantise_unit(h_raw[u], h_codes[:, :, unit_rows(u)], h_scales[:, :, unit_rows(u)], engines)
 
-        def quantise_w(l):
+        def quantise_w(l, engines=("scalar", "scalar")):
             for u in range(UNITS):
-                quantise_unit(w_raw[(l, u)], w_codes[:, l, :, unit_rows(u)], w_scales[:, l, :, unit_rows(u)])
+                quantise_unit(w_raw[(l, u)], w_codes[:, l, :, unit_rows(u)], w_scales[:, l, :, unit_rows(u)], engines)
 
-        quantise_h(0)
+        both = ("vector", "scalar")
+        quantise_h(0, both)
 
-        bias_bc = const.tile([P, L, H], BF16)
-        for l in range(L):
+        def spread_row(row, target):
             for half in range(HALVES):
                 cols = slice(half * BANK, (half + 1) * BANK)
                 spread = psum.tile([P, BANK], F32, tag="t")
                 nc.tensor.matmul(
-                    out=spread[:], lhsT=ident_bf16[:, l : l + 1].to_broadcast([P, P]), rhs=rows[:, cols],
+                    out=spread[:], lhsT=ident_bf16[:, row : row + 1].to_broadcast([P, P]), rhs=rows[:, cols],
                     start=True, stop=True,
                 )
-                nc.scalar.copy(out=bias_bc[:, l, cols], in_=spread[:])
+                nc.scalar.copy(out=target[:, cols], in_=spread[:])
+
+        bias_bc = const.tile([P, L, H], BF16)
+        last_gain_bc = const.tile([P, H], BF16)
+        spread_row(0, bias_bc[:, 0, :])
+        quantise_w(0, both)
+        for l in range(1, L):
+            spread_row(l, bias_bc[:, l, :])
         rows_T = psum.tile([P, N_TILES, P], BF16, tag="t")
         for t in range(N_TILES):
             nc.tensor.transpose(rows_T[:, t, :], rows[:, t * P : (t + 1) * P], ident_bf16[:])
@@ -128,11 +142,10 @@ def tile_advancedliquidneuralnetwork_pa_kernel(tc, h, W_liq, b_liq, g_liq, beta_
         shift_T = const.tile([P, N_TILES], F32)
         nc.vector.tensor_reduce(out=shift_T[:], in_=params_T[:, :, 2 * L : 3 * L], axis=mybir.AxisListType.X, op=ADD)
 
-        def normalised_branch(l, u, j):
+        def branch(l, u, j):
             tile_cols = slice((u * UNIT_TILES + j) * P, (u * UNIT_TILES + j + 1) * P)
-            resid = work.tile([P, H], F32, bufs=6)
-            nc.vector.tensor_tensor(out=resid[:], in0=h_raw[u][:, j, :], in1=bias_bc[:, l, :], op=ADD)
-            pre = work.tile([P, H], F32)
+            pre = work.tile([P, H], F32, name="pre", bufs=12)
+            nc.vector.tensor_tensor(out=pre[:], in0=h_raw[u][:, j, :], in1=bias_bc[:, l, :], op=ADD)
             row_sum = stats.tile([P, HALVES], F32)
             for half in range(HALVES):
                 cols = slice(half * BANK, (half + 1) * BANK)
@@ -148,24 +161,36 @@ def tile_advancedliquidneuralnetwork_pa_kernel(tc, h, W_liq, b_liq, g_liq, beta_
                         stop=(c == PASSES - 1),
                     )
                 nc.vector.scalar_tensor_tensor(
-                    out=pre[:, cols], in0=resid[:, cols], scalar=0.0, in1=product[:],
+                    out=pre[:, cols], in0=pre[:, cols], scalar=0.0, in1=product[:],
                     op0=ADD, op1=ADD, accum_out=row_sum[:, half : half + 1],
                 )
             neg_mean = stats.tile([P, 1], F32)
             nc.vector.tensor_scalar(
                 out=neg_mean[:], in0=row_sum[:, 0:1], scalar1=row_sum[:, 1:2], scalar2=-1.0 / H, op0=ADD, op1=MULT
             )
-            z = z_pool.tile([P, H], F32)
+            squares = work.tile([P, H], BF16, name="squares", bufs=2)
             sum_sq = stats.tile([P, 1], F32)
-            nc.scalar.activation(out=z[:], in_=pre[:], func=ACT.Square, bias=neg_mean[:], scale=1.0, accum_out=sum_sq[:])
-            std = stats.tile([P, 1], F32)
-            nc.scalar.activation(out=std[:], in_=sum_sq[:], func=ACT.Sqrt, bias=eps[:], scale=1.0 / H)
+            nc.scalar.activation(
+                out=squares[:], in_=pre[:], func=ACT.Square, bias=neg_mean[:], scale=1.0, accum_out=sum_sq[:]
+            )
             rstd = stats.tile([P, 1], F32)
-            nc.vector.reciprocal(rstd[:], std[:])
-            nc.gpsimd.tensor_scalar(out=z[:], in0=pre[:], scalar1=neg_mean[:], scalar2=rstd[:], op0=ADD, op1=MULT)
-            return z
+            nc.scalar.activation(
+                out=rstd[:], in_=sum_sq[:], func=ACT.Abs_reciprocal_sqrt, bias=eps[:], scale=1.0 / H
+            )
+            return pre, neg_mean, rstd
 
-        def add_branch(l, zs, acc_T):
+        y_Ts = {}
+
+        def normalised(l, u, j):
+            pre, neg_mean, rstd = branch(l, u, j)
+            nc.gpsimd.tensor_scalar(out=pre[:], in0=pre[:], scalar1=neg_mean[:], scalar2=rstd[:], op0=ADD, op1=MULT)
+            return pre
+
+        def gains(l, u, zs):
+            join = 0 and l == 1
+            if not join:
+                y_Ts[(u, l)] = gained.tile([P, N_TILES, UNIT_ROWS], F32, name="y_T%d" % l)
+            y_T = y_Ts[(u, 0 if join else l)]
             for t in range(N_TILES):
                 z_T = psum.tile([P, UNIT_TILES, P], F32, tag="t")
                 for j in range(UNIT_TILES):
@@ -174,47 +199,59 @@ def tile_advancedliquidneuralnetwork_pa_kernel(tc, h, W_liq, b_liq, g_liq, beta_
                 gain = params_T[:, t, L + l : L + l + 1]
                 if l == 0:
                     nc.scalar.activation(
-                        out=acc_T[:, t, :], in_=z_T_cols, func=ACT.Identity, bias=shift_T[:, t : t + 1], scale=gain
+                        out=y_T[:, t, :], in_=z_T_cols, func=ACT.Identity, bias=shift_T[:, t : t + 1], scale=gain
+                    )
+                elif join:
+                    nc.vector.scalar_tensor_tensor(
+                        out=y_T[:, t, :], in0=z_T_cols, scalar=gain, in1=y_T[:, t, :], op0=MULT, op1=ADD
                     )
                 else:
-                    nc.vector.scalar_tensor_tensor(
-                        out=acc_T[:, t, :], in0=z_T_cols, scalar=gain, in1=acc_T[:, t, :], op0=MULT, op1=ADD
-                    )
+                    nc.scalar.activation(out=y_T[:, t, :], in_=z_T_cols, func=ACT.Copy, scale=gain)
 
-        def store_unit(u, acc_T):
-            for j in range(UNIT_TILES):
-                result = out_pool.tile([P, H], F32)
-                for half in range(HALVES):
-                    rows_back = psum.tile([P, BANK_TILES, P], F32, tag="t")
-                    for t in range(BANK_TILES):
-                        nc.tensor.transpose(
-                            rows_back[:, t, :], acc_T[:, half * BANK_TILES + t, j * P : (j + 1) * P], ident_f32[:]
+        def last_branch(u, j):
+            pre, neg_mean, rstd = branch(L - 1, u, j)
+            result = out_pool.tile([P, H], F32, name="result")
+            nc.vector.scalar_tensor_tensor(
+                out=result[:], in0=pre[:], scalar=neg_mean[:], in1=last_gain_bc[:], op0=ADD, op1=MULT
+            )
+            parts = [l for l in range(L - 1) if (u, l) in y_Ts]
+            first = (u * UNIT_TILES + j) * P
+            for half in range(HALVES):
+                summed = psum.tile([P, BANK_TILES, P], F32, tag="t")
+                for t in range(BANK_TILES):
+                    for n, l in enumerate(parts):
+                        nc.tensor.matmul(
+                            out=summed[:, t, :],
+                            lhsT=y_Ts[(u, l)][:, half * BANK_TILES + t, j * P : (j + 1) * P],
+                            rhs=ident_f32[:],
+                            is_transpose=True,
+                            start=(n == 0),
+                            stop=(n == len(parts) - 1),
                         )
-                    nc.scalar.copy(
-                        out=result[:, half * BANK : (half + 1) * BANK], in_=rows_back[:].rearrange("p t n -> p (t n)")
-                    )
-                first = (u * UNIT_TILES + j) * P
-                nc.sync.dma_start(out=out[first : first + P, :], in_=result[:])
+                cols = slice(half * BANK, (half + 1) * BANK)
+                nc.vector.scalar_tensor_tensor(
+                    out=result[:, cols], in0=result[:, cols], scalar=rstd[:],
+                    in1=summed[:].rearrange("p t n -> p (t n)"), op0=MULT, op1=ADD,
+                )
+                nc.sync.dma_start(out=out[first : first + P, cols], in_=result[:, cols])
 
-        acc_Ts = {}
-
-        def finish(u, l, zs):
-            if l == 0:
-                acc_Ts[u] = acc_pool.tile([P, N_TILES, UNIT_ROWS], F32, name="acc_T")
-            add_branch(l, zs, acc_Ts[u])
-            if l == L - 1:
-                store_unit(u, acc_Ts[u])
-
-        quantise_w(0)
+        steps = [(u, l) for u in range(UNITS) for l in range(L - 1)]
         waiting = None
+        for s, (u, l) in enumerate(steps):
+            if s == 0:
+                quantise_w(1)
+            elif s == 1:
+                quantise_h(1)
+            elif s == 2:
+                quantise_w(2)
+            zs = [normalised(l, u, j) for j in range(UNIT_TILES)]
+            if waiting is not None:
+                gains(*waiting)
+            waiting = (l, u, zs)
+        spread_row(L + L - 1, last_gain_bc[:])
         for u in range(UNITS):
-            for l in range(L):
-                if u == 0 and l + 1 < L:
-                    quantise_w(l + 1)
-                if u + 1 < UNITS and l == L - 1:
-                    quantise_h(u + 1)
-                zs = [normalised_branch(l, u, j) for j in range(UNIT_TILES)]
-                if waiting is not None:
-                    finish(*waiting)
-                waiting = (u, l, zs)
-        finish(*waiting)
+            for j in range(UNIT_TILES):
+                last_branch(u, j)
+            if waiting is not None:
+                gains(*waiting)
+                waiting = None

@@ -68,7 +68,7 @@ def tile_advancedliquidneuralnetwork_pa_kernel(tc, h, W_liq, b_liq, g_liq, beta_
             if l == L - 1:
                 h_raw[1] = load_unit("h_raw", UNITS, h[unit_rows(1), :], 1)
             for u in range(UNITS):
-                w_raw[(l, u)] = load_unit("w_raw", 3, W_liq[l, unit_rows(u), :], 2 if l == 0 else 1)
+                w_raw[(l, u)] = load_unit("w_raw", 4, W_liq[l, unit_rows(u), :], 2 if l == 0 else 1)
 
         ident_f32 = const.tile([P, P], F32)
         make_identity(nc, ident_f32[:])
@@ -144,7 +144,7 @@ def tile_advancedliquidneuralnetwork_pa_kernel(tc, h, W_liq, b_liq, g_liq, beta_
 
         def branch(l, u, j):
             tile_cols = slice((u * UNIT_TILES + j) * P, (u * UNIT_TILES + j + 1) * P)
-            pre = work.tile([P, H], F32, name="pre", bufs=12)
+            pre = work.tile([P, H], F32, name="pre", bufs=13)
             nc.vector.tensor_tensor(out=pre[:], in0=h_raw[u][:, j, :], in1=bias_bc[:, l, :], op=ADD)
             row_sum = stats.tile([P, HALVES], F32)
             for half in range(HALVES):
@@ -187,7 +187,7 @@ def tile_advancedliquidneuralnetwork_pa_kernel(tc, h, W_liq, b_liq, g_liq, beta_
             return pre
 
         def gains(l, u, zs):
-            join = 0 and l == 1
+            join = 1 and l == 1
             if not join:
                 y_Ts[(u, l)] = gained.tile([P, N_TILES, UNIT_ROWS], F32, name="y_T%d" % l)
             y_T = y_Ts[(u, 0 if join else l)]

@@ -58,7 +58,7 @@ def tile_advancedliquidneuralnetwork_pa_kernel(tc, h, W_liq, b_liq, g_liq, beta_
 
         h_raw = [None] * UNITS
         w_raw = {}
-        h_raw[0] = load_unit("h_raw", UNITS, h[unit_rows(0), :], 2)
+        h_raw[0] = load_unit("h_raw", UNITS, h[unit_rows(0), :], 4)
         rows = const.tile([P, H], BF16)
         nc.vector.memset(rows[:].bitcast(I32), 0)
         nc.sync.dma_start(out=rows[0:L, :], in_=b_liq)
@@ -68,7 +68,7 @@ def tile_advancedliquidneuralnetwork_pa_kernel(tc, h, W_liq, b_liq, g_liq, beta_
             if l == L - 1:
                 h_raw[1] = load_unit("h_raw", UNITS, h[unit_rows(1), :], 1)
             for u in range(UNITS):
-                w_raw[(l, u)] = load_unit("w_raw", 4, W_liq[l, unit_rows(u), :], 2 if l == 0 else 1)
+                w_raw[(l, u)] = load_unit("w_raw", 3, W_liq[l, unit_rows(u), :], 4 if l == 0 else 1)
 
         ident_f32 = const.tile([P, P], F32)
         make_identity(nc, ident_f32[:])
@@ -79,10 +79,10 @@ def tile_advancedliquidneuralnetwork_pa_kernel(tc, h, W_liq, b_liq, g_liq, beta_
         warm = const.tile([P, 1], F32)
         nc.scalar.activation(out=warm[:], in_=eps[:], func=ACT.Abs_reciprocal_sqrt)
 
-        h_codes = keep.tile([P, PASSES, B], U32, align_bytes=64)
-        h_scales = keep.tile([P, PASSES, B], U8, align_bytes=64)
-        w_codes = keep.tile([P, L, PASSES, H], U32, align_bytes=64)
-        w_scales = keep.tile([P, L, PASSES, H], U8, align_bytes=64)
+        h_codes = keep.tile([P, UNITS, PASSES, UNIT_ROWS], U32, align_bytes=64)
+        h_scales = keep.tile([P, UNITS, PASSES, UNIT_ROWS], U8, align_bytes=64)
+        w_codes = keep.tile([P, L, UNITS, PASSES, UNIT_ROWS], U32, align_bytes=64)
+        w_scales = keep.tile([P, L, UNITS, PASSES, UNIT_ROWS], U8, align_bytes=64)
 
         def quantise_unit(raw, codes, scales, engines):
             grouped = stage.tile([P, PASSES, UNIT_TILES, P, PACK], BF16, align_bytes=64)
@@ -101,19 +101,18 @@ def tile_advancedliquidneuralnetwork_pa_kernel(tc, h, W_liq, b_liq, g_liq, beta_
                     nc.vector.tensor_copy(out=grouped_words[:, :, j, :, :], in_=words)
                 else:
                     nc.scalar.copy(out=grouped_words[:, :, j, :, :], in_=words)
-            for c in range(PASSES):
-                nc.vector.quantize_mx(
-                    out=codes[:, c, :].bitcast(FP8X4),
-                    scales=scales[:, c, :],
-                    in_=grouped[:, c].rearrange("p j r t -> p (j r t)"),
-                )
+            nc.vector.quantize_mx(
+                out=codes.rearrange("p c r -> p (c r)").bitcast(FP8X4),
+                scales=scales.rearrange("p c r -> p (c r)"),
+                in_=grouped[:].rearrange("p c j r t -> p (c j r t)"),
+            )
 
         def quantise_h(u, engines=("scalar", "scalar")):
-            quantise_unit(h_raw[u], h_codes[:, :, unit_rows(u)], h_scales[:, :, unit_rows(u)], engines)
+            quantise_unit(h_raw[u], h_codes[:, u], h_scales[:, u], engines)
 
         def quantise_w(l, engines=("scalar", "scalar")):
             for u in range(UNITS):
-                quantise_unit(w_raw[(l, u)], w_codes[:, l, :, unit_rows(u)], w_scales[:, l, :, unit_rows(u)], engines)
+                quantise_unit(w_raw[(l, u)], w_codes[:, l, u], w_scales[:, l, u], engines)
 
         both = ("vector", "scalar")
         quantise_h(0, both)
@@ -143,9 +142,10 @@ def tile_advancedliquidneuralnetwork_pa_kernel(tc, h, W_liq, b_liq, g_liq, beta_
         nc.vector.tensor_reduce(out=shift_T[:], in_=params_T[:, :, 2 * L : 3 * L], axis=mybir.AxisListType.X, op=ADD)
 
         def branch(l, u, j):
-            tile_cols = slice((u * UNIT_TILES + j) * P, (u * UNIT_TILES + j + 1) * P)
-            pre = work.tile([P, H], F32, name="pre", bufs=13)
-            nc.vector.tensor_tensor(out=pre[:], in0=h_raw[u][:, j, :], in1=bias_bc[:, l, :], op=ADD)
+            tile_cols = slice(j * P, (j + 1) * P)
+            pre = work.tile([P, H], F32, name="pre", bufs=12)
+            adder = nc.gpsimd if l == L - 1 and (u > 0 or j in (3,)) else nc.vector
+            adder.tensor_tensor(out=pre[:], in0=h_raw[u][:, j, :], in1=bias_bc[:, l, :], op=ADD)
             row_sum = stats.tile([P, HALVES], F32)
             for half in range(HALVES):
                 cols = slice(half * BANK, (half + 1) * BANK)
@@ -153,10 +153,10 @@ def tile_advancedliquidneuralnetwork_pa_kernel(tc, h, W_liq, b_liq, g_liq, beta_
                 for c in range(PASSES):
                     nc.tensor.matmul_mx(
                         out=product[:],
-                        lhsT=h_codes[:, c, tile_cols].bitcast(FP8X4),
-                        lhsT_scale=h_scales[:, c, tile_cols],
-                        rhs=w_codes[:, l, c, cols].bitcast(FP8X4),
-                        rhs_scale=w_scales[:, l, c, cols],
+                        lhsT=h_codes[:, u, c, tile_cols].bitcast(FP8X4),
+                        lhsT_scale=h_scales[:, u, c, tile_cols],
+                        rhs=w_codes[:, l, half, c, :].bitcast(FP8X4),
+                        rhs_scale=w_scales[:, l, half, c, :],
                         start=(c == 0),
                         stop=(c == PASSES - 1),
                     )
@@ -186,12 +186,12 @@ def tile_advancedliquidneuralnetwork_pa_kernel(tc, h, W_liq, b_liq, g_liq, beta_
             nc.gpsimd.tensor_scalar(out=pre[:], in0=pre[:], scalar1=neg_mean[:], scalar2=rstd[:], op0=ADD, op1=MULT)
             return pre
 
-        def gains(l, u, zs):
-            join = 1 and l == 1
-            if not join:
+        def gains(l, u, zs, tiles=range(N_TILES)):
+            join = 0 and l == 1
+            if not join and tiles[0] == 0:
                 y_Ts[(u, l)] = gained.tile([P, N_TILES, UNIT_ROWS], F32, name="y_T%d" % l)
             y_T = y_Ts[(u, 0 if join else l)]
-            for t in range(N_TILES):
+            for t in tiles:
                 z_T = psum.tile([P, UNIT_TILES, P], F32, tag="t")
                 for j in range(UNIT_TILES):
                     nc.tensor.transpose(z_T[:, j, :], zs[j][:, t * P : (t + 1) * P], ident_f32[:])
@@ -242,16 +242,16 @@ def tile_advancedliquidneuralnetwork_pa_kernel(tc, h, W_liq, b_liq, g_liq, beta_
                 quantise_w(1)
             elif s == 1:
                 quantise_h(1)
+                spread_row(L + L - 1, last_gain_bc[:])
             elif s == 2:
                 quantise_w(2)
             zs = [normalised(l, u, j) for j in range(UNIT_TILES)]
             if waiting is not None:
                 gains(*waiting)
             waiting = (l, u, zs)
-        spread_row(L + L - 1, last_gain_bc[:])
         for u in range(UNITS):
             for j in range(UNIT_TILES):
+                if u == 0:
+                    share = N_TILES // UNIT_TILES
+                    gains(*waiting, tiles=range(j * share, (j + 1) * share))
                 last_branch(u, j)
-            if waiting is not None:
-                gains(*waiting)
-                waiting = None

from contextlib import ExitStack

import concourse.mybir as mybir
from concourse.masks import make_identity

F32 = mybir.dt.float32
BF16 = mybir.dt.bfloat16
U32 = mybir.dt.uint32
U8 = mybir.dt.uint8
I32 = mybir.dt.int32
FP8X4 = mybir.dt.float8_e4m3fn_x4
ADD = mybir.AluOpType.add
MULT = mybir.AluOpType.mult
ACT = mybir.ActivationFunctionType

P = 128
B = 1024
H = 1024
L = 3
LN_EPS = 1e-5
PACK = 4
K_PASS = P * PACK
PASSES = H // K_PASS
BANK = 512
HALVES = H // BANK
UNIT_TILES = 4
UNIT_ROWS = UNIT_TILES * P
UNITS = B // UNIT_ROWS
N_TILES = H // P
BANK_TILES = BANK // P

FLOPS = 2 * L * B * H * H


def tile_advancedliquidneuralnetwork_pa_kernel(tc, h, W_liq, b_liq, g_liq, beta_liq, out):
    nc = tc.nc
    with ExitStack() as ctx:
        const = ctx.enter_context(tc.tile_pool(name="const", bufs=1))
        raw_pool = ctx.enter_context(tc.tile_pool(name="raw", bufs=1))
        stage = ctx.enter_context(tc.tile_pool(name="stage", bufs=2))
        keep = ctx.enter_context(tc.tile_pool(name="keep", bufs=1))
        work = ctx.enter_context(tc.tile_pool(name="work", bufs=1))
        gained = ctx.enter_context(tc.tile_pool(name="gained", bufs=2))
        out_pool = ctx.enter_context(tc.tile_pool(name="result", bufs=3))
        stats = ctx.enter_context(tc.tile_pool(name="stats", bufs=8))
        psum = ctx.enter_context(tc.psum_pool(name="psum", bufs=4))

        def load_unit(name, slots, dram_rows, pieces):
            raw = raw_pool.tile([P, UNIT_TILES, H], BF16, name=name, bufs=slots)
            source = dram_rows.rearrange("(j p) k -> p j k", p=P)
            step = UNIT_TILES // pieces
            for first in range(0, UNIT_TILES, step):
                nc.sync.dma_start(out=raw[:, first : first + step, :], in_=source[:, first : first + step, :])
            return raw

        def unit_rows(u):
            return slice(u * UNIT_ROWS, (u + 1) * UNIT_ROWS)

        h_raw = [None] * UNITS
        w_raw = {}
        h_raw[0] = load_unit("h_raw", UNITS, h[unit_rows(0), :], 4)
        rows = const.tile([P, H], BF16)
        nc.vector.memset(rows[:].bitcast(I32), 0)
        nc.sync.dma_start(out=rows[0:L, :], in_=b_liq)
        nc.sync.dma_start(out=rows[L : 2 * L, :], in_=g_liq)
        nc.sync.dma_start(out=rows[2 * L : 3 * L, :], in_=beta_liq)
        for l in range(L):
            if l == L - 1:
                h_raw[1] = load_unit("h_raw", UNITS, h[unit_rows(1), :], 1)
            for u in range(UNITS):
                w_raw[(l, u)] = load_unit("w_raw", 3, W_liq[l, unit_rows(u), :], 4 if l == 0 else 1)

        ident_f32 = const.tile([P, P], F32)
        make_identity(nc, ident_f32[:])
        ident_bf16 = const.tile([P, P], BF16)
        make_identity(nc, ident_bf16[:])
        eps = const.tile([P, 1], F32)
        nc.vector.memset(eps[:], LN_EPS)
        warm = const.tile([P, 1], F32)
        nc.scalar.activation(out=warm[:], in_=eps[:], func=ACT.Abs_reciprocal_sqrt)

        h_codes = keep.tile([P, UNITS, PASSES, UNIT_ROWS], U32, align_bytes=64)
        h_scales = keep.tile([P, UNITS, PASSES, UNIT_ROWS], U8, align_bytes=64)
        w_codes = keep.tile([P, L, UNITS, PASSES, UNIT_ROWS], U32, align_bytes=64)
        w_scales = keep.tile([P, L, UNITS, PASSES, UNIT_ROWS], U8, align_bytes=64)

        def quantise_unit(raw, codes, scales, engines):
            grouped = stage.tile([P, PASSES, UNIT_TILES, P, PACK], BF16, align_bytes=64)
            grouped_words = grouped[:].bitcast(F32)
            for j in range(UNIT_TILES):
                raw_words = raw[:, j, :].bitcast(F32)
                flipped = psum.tile([P, PASSES, 2, P], F32, tag="t")
                for c in range(PASSES):
                    for w in range(2):
                        first = 2 * c * P + w
                        nc.tensor.transpose(
                            flipped[:, c, w, :], raw_words[:, first : 2 * (c + 1) * P : 2], ident_f32[:]
                        )
                words = flipped[:].rearrange("p c w r -> p c r w")
                if engines[j % 2] == "vector":
                    nc.vector.tensor_copy(out=grouped_words[:, :, j, :, :], in_=words)
                else:
                    nc.scalar.copy(out=grouped_words[:, :, j, :, :], in_=words)
            nc.vector.quantize_mx(
                out=codes.rearrange("p c r -> p (c r)").bitcast(FP8X4),
                scales=scales.rearrange("p c r -> p (c r)"),
                in_=grouped[:].rearrange("p c j r t -> p (c j r t)"),
            )

        def quantise_h(u, engines=("scalar", "scalar")):
            quantise_unit(h_raw[u], h_codes[:, u], h_scales[:, u], engines)

        def quantise_w(l, engines=("scalar", "scalar")):
            for u in range(UNITS):
                quantise_unit(w_raw[(l, u)], w_codes[:, l, u], w_scales[:, l, u], engines)

        both = ("vector", "scalar")
        quantise_h(0, both)

        def spread_row(row, target):
            for half in range(HALVES):
                cols = slice(half * BANK, (half + 1) * BANK)
                spread = psum.tile([P, BANK], F32, tag="t")
                nc.tensor.matmul(
                    out=spread[:], lhsT=ident_bf16[:, row : row + 1].to_broadcast([P, P]), rhs=rows[:, cols],
                    start=True, stop=True,
                )
                nc.scalar.copy(out=target[:, cols], in_=spread[:])

        bias_bc = const.tile([P, L, H], BF16)
        last_gain_bc = const.tile([P, H], BF16)
        spread_row(0, bias_bc[:, 0, :])
        quantise_w(0, both)
        for l in range(1, L):
            spread_row(l, bias_bc[:, l, :])
        rows_T = psum.tile([P, N_TILES, P], BF16, tag="t")
        for t in range(N_TILES):
            nc.tensor.transpose(rows_T[:, t, :], rows[:, t * P : (t + 1) * P], ident_bf16[:])
        params_T = const.tile([P, N_TILES, 3 * L], F32)
        nc.vector.tensor_copy(out=params_T[:], in_=rows_T[:, :, 0 : 3 * L])
        shift_T = const.tile([P, N_TILES], F32)
        nc.vector.tensor_reduce(out=shift_T[:], in_=params_T[:, :, 2 * L : 3 * L], axis=mybir.AxisListType.X, op=ADD)

        def branch(l, u, j):
            tile_cols = slice(j * P, (j + 1) * P)
            pre = work.tile([P, H], F32, name="pre", bufs=12)
            adder = nc.gpsimd if l == L - 1 and (u > 0 or j in (3,)) else nc.vector
            adder.tensor_tensor(out=pre[:], in0=h_raw[u][:, j, :], in1=bias_bc[:, l, :], op=ADD)
            row_sum = stats.tile([P, HALVES], F32)
            for half in range(HALVES):
                cols = slice(half * BANK, (half + 1) * BANK)
                product = psum.tile([P, BANK], F32, tag="x")
                for c in range(PASSES):
                    nc.tensor.matmul_mx(
                        out=product[:],
                        lhsT=h_codes[:, u, c, tile_cols].bitcast(FP8X4),
                        lhsT_scale=h_scales[:, u, c, tile_cols],
                        rhs=w_codes[:, l, half, c, :].bitcast(FP8X4),
                        rhs_scale=w_scales[:, l, half, c, :],
                        start=(c == 0),
                        stop=(c == PASSES - 1),
                    )
                nc.vector.scalar_tensor_tensor(
                    out=pre[:, cols], in0=pre[:, cols], scalar=0.0, in1=product[:],
                    op0=ADD, op1=ADD, accum_out=row_sum[:, half : half + 1],
                )
            neg_mean = stats.tile([P, 1], F32)
            nc.vector.tensor_scalar(
                out=neg_mean[:], in0=row_sum[:, 0:1], scalar1=row_sum[:, 1:2], scalar2=-1.0 / H, op0=ADD, op1=MULT
            )
            squares = work.tile([P, H], BF16, name="squares", bufs=2)
            sum_sq = stats.tile([P, 1], F32)
            nc.scalar.activation(
                out=squares[:], in_=pre[:], func=ACT.Square, bias=neg_mean[:], scale=1.0, accum_out=sum_sq[:]
            )
            rstd = stats.tile([P, 1], F32)
            nc.scalar.activation(
                out=rstd[:], in_=sum_sq[:], func=ACT.Abs_reciprocal_sqrt, bias=eps[:], scale=1.0 / H
            )
            return pre, neg_mean, rstd

        y_Ts = {}

        def normalised(l, u, j):
            pre, neg_mean, rstd = branch(l, u, j)
            nc.gpsimd.tensor_scalar(out=pre[:], in0=pre[:], scalar1=neg_mean[:], scalar2=rstd[:], op0=ADD, op1=MULT)
            return pre

        def gains(l, u, zs, tiles=range(N_TILES)):
            join = 0 and l == 1
            if not join and tiles[0] == 0:
                y_Ts[(u, l)] = gained.tile([P, N_TILES, UNIT_ROWS], F32, name="y_T%d" % l)
            y_T = y_Ts[(u, 0 if join else l)]
            for t in tiles:
                z_T = psum.tile([P, UNIT_TILES, P], F32, tag="t")
                for j in range(UNIT_TILES):
                    nc.tensor.transpose(z_T[:, j, :], zs[j][:, t * P : (t + 1) * P], ident_f32[:])
                z_T_cols = z_T[:].rearrange("p j r -> p (j r)")
                gain = params_T[:, t, L + l : L + l + 1]
                if l == 0:
                    nc.scalar.activation(
                        out=y_T[:, t, :], in_=z_T_cols, func=ACT.Identity, bias=shift_T[:, t : t + 1], scale=gain
                    )
                elif join:
                    nc.vector.scalar_tensor_tensor(
                        out=y_T[:, t, :], in0=z_T_cols, scalar=gain, in1=y_T[:, t, :], op0=MULT, op1=ADD
                    )
                else:
                    nc.scalar.activation(out=y_T[:, t, :], in_=z_T_cols, func=ACT.Copy, scale=gain)

        def last_branch(u, j):
            pre, neg_mean, rstd = branch(L - 1, u, j)
            result = out_pool.tile([P, H], F32, name="result")
            nc.vector.scalar_tensor_tensor(
                out=result[:], in0=pre[:], scalar=neg_mean[:], in1=last_gain_bc[:], op0=ADD, op1=MULT
            )
            parts = [l for l in range(L - 1) if (u, l) in y_Ts]
            first = (u * UNIT_TILES + j) * P
            for half in range(HALVES):
                summed = psum.tile([P, BANK_TILES, P], F32, tag="t")
                for t in range(BANK_TILES):
                    for n, l in enumerate(parts):
                        nc.tensor.matmul(
                            out=summed[:, t, :],
                            lhsT=y_Ts[(u, l)][:, half * BANK_TILES + t, j * P : (j + 1) * P],
                            rhs=ident_f32[:],
                            is_transpose=True,
                            start=(n == 0),
                            stop=(n == len(parts) - 1),
                        )
                cols = slice(half * BANK, (half + 1) * BANK)
                nc.vector.scalar_tensor_tensor(
                    out=result[:, cols], in0=result[:, cols], scalar=rstd[:],
                    in1=summed[:].rearrange("p t n -> p (t n)"), op0=MULT, op1=ADD,
                )
                nc.sync.dma_start(out=out[first : first + P, cols], in_=result[:, cols])

        steps = [(u, l) for u in range(UNITS) for l in range(L - 1)]
        waiting = None
        for s, (u, l) in enumerate(steps):
            if s == 0:
                quantise_w(1)
            elif s == 1:
                quantise_h(1)
                spread_row(L + L - 1, last_gain_bc[:])
            elif s == 2:
                quantise_w(2)
            zs = [normalised(l, u, j) for j in range(UNIT_TILES)]
            if waiting is not None:
                gains(*waiting)
            waiting = (l, u, zs)
        for u in range(UNITS):
            for j in range(UNIT_TILES):
                if u == 0:
                    share = N_TILES // UNIT_TILES
                    gains(*waiting, tiles=range(j * share, (j + 1) * share))
                last_branch(u, j)
